import numpy as np
import ml_dtypes

BF16 = ml_dtypes.bfloat16


def bf(x):
    return np.asarray(x, np.float32).astype(BF16)


def f32(x):
    return np.asarray(x, np.float32)


def f64(x):
    return np.asarray(x).astype(np.float64)


def striped(idx):
    return np.tile(idx.reshape(-1, 16).T, (8, 1))


CIN, H, C, S, N, DEG = 1024, 512, 256, 4096, 1024, 8


def setup_inputs():
    base = f32(np.random.standard_normal((C, S)))
    x = bf(np.random.standard_normal((CIN, N)))
    adj_t = bf((np.random.random((N, N)) < DEG / N) * np.random.random((N, N)) * np.sqrt(3.0 / DEG))
    w1 = bf(np.random.standard_normal((CIN, H)) / np.sqrt(CIN))
    w2 = bf(np.random.standard_normal((H, H)) / np.sqrt(H))
    w3 = bf(np.random.standard_normal((H, C)) / np.sqrt(H))
    return {"base": base, "x": x, "adj_t": adj_t, "w1": w1, "w2": w2, "w3": w3, "offs": striped(np.random.permutation(S)[:N])}


def reference(base, x, adj_t, w1, w2, w3, offs):
    idx = offs[:16].T.reshape(-1)
    a = f64(adj_t)
    z = f64(x)
    for w in (w1, w2):
        y = z.T @ f64(w)
        z = np.maximum(y.T @ a, 0.0)
    y = z.T @ f64(w3)
    v = y.T @ a
    out = f64(base).copy()
    out[:, idx] = v * (v > 0)
    return out

@@ -1,0 +1,93 @@
+import concourse.mybir as mybir
+
+P = 128
+CIN, H, C, S, N = 1024, 512, 256, 4096, 1024
+BANK = 512
+FLOPS = 2 * (N * CIN * H + H * N * N + N * H * H + H * N * N + N * H * C + C * N * N)
+
+BF16, F32, U16 = mybir.dt.bfloat16, mybir.dt.float32, mybir.dt.uint16
+COPY, RELU = mybir.ActivationFunctionType.Copy, mybir.ActivationFunctionType.Relu
+MULT, IS_GT = mybir.AluOpType.mult, mybir.AluOpType.is_gt
+
+
+def load_row_block(nc, pool, matrix, block, name):
+    rows = pool.tile([P, matrix.shape[1]], matrix.dtype, name=f"{name}{block}")
+    nc.sync.dma_start(rows[:], matrix[block * P : (block + 1) * P, :])
+    return rows
+
+
+def leave_psum(nc, turn, dest, bank, relu):
+    if turn % 2 == 0:
+        nc.scalar.activation(dest, bank, RELU if relu else COPY)
+    elif relu:
+        nc.vector.tensor_scalar_max(dest, bank, 0.0)
+    else:
+        nc.vector.tensor_copy(dest, bank)
+
+
+def times_weights(nc, held, banks, z, w, name):
+    width = w[0].shape[1]
+    y = []
+    for m in range(N // P):
+        acc = banks.tile([P, width], F32, name="acc")
+        for k in range(len(z)):
+            nc.tensor.matmul(acc[:], z[k][:, m * P : (m + 1) * P], w[k][:], start=(k == 0), stop=(k == len(z) - 1))
+        y_m = held.tile([P, width], BF16, name=f"{name}{m}")
+        leave_psum(nc, m, y_m[:], acc[:], relu=False)
+        y.append(y_m)
+    return y
+
+
+def times_adjacency(nc, banks, y, adj, block, half):
+    acc = banks.tile([P, BANK], F32, name="acc")
+    for m in range(N // P):
+        nc.tensor.matmul(
+            acc[:],
+            y[m][:, block * P : (block + 1) * P],
+            adj[m][:, half * BANK : (half + 1) * BANK],
+            start=(m == 0),
+            stop=(m == N // P - 1),
+        )
+    return acc
+
+
+def hidden_layer(nc, held, banks, z, w, adj, name):
+    y = times_weights(nc, held, banks, z, w, f"y{name}_")
+    z_next = [held.tile([P, N], BF16, name=f"z{name}_{h}") for h in range(H // P)]
+    for half in range(N // BANK):
+        for h in range(H // P):
+            acc = times_adjacency(nc, banks, y, adj, h, half)
+            leave_psum(nc, h, z_next[h][:, half * BANK : (half + 1) * BANK], acc[:], relu=True)
+    return z_next
+
+
+def tile_gae_b_kernel(tc, base, x, adj_t, w1, w2, w3, offs, out):
+    nc = tc.nc
+    with (
+        tc.tile_pool(name="held", bufs=1) as held,
+        tc.psum_pool(name="banks", bufs=8) as banks,
+    ):
+        offsets = held.tile([P, N // 16], U16, name="offsets")
+        nc.sync.dma_start(offsets[:], offs)
+        x_k, w1_k = [], []
+        for k in range(CIN // P):
+            x_k.append(load_row_block(nc, held, x, k, "x"))
+            w1_k.append(load_row_block(nc, held, w1, k, "w1_"))
+        adj = [load_row_block(nc, held, adj_t, m, "adj") for m in range(N // P)]
+        w2_k = [load_row_block(nc, held, w2, k, "w2_") for k in range(H // P)]
+        w3_k = [load_row_block(nc, held, w3, k, "w3_") for k in range(H // P)]
+        window = [load_row_block(nc, held, base, c, "window") for c in range(C // P)]
+
+        z1 = hidden_layer(nc, held, banks, x_k, w1_k, adj, "1")
+        z2 = hidden_layer(nc, held, banks, z1, w2_k, adj, "2")
+        y3 = times_weights(nc, held, banks, z2, w3_k, "y3_")
+
+        for c in range(C // P):
+            v = held.tile([P, N], F32, name=f"v{c}")
+            pos = held.tile([P, N], F32, name=f"pos{c}")
+            for half in range(N // BANK):
+                acc = times_adjacency(nc, banks, y3, adj, c, half)
+                nc.scalar.activation(v[:, half * BANK : (half + 1) * BANK], acc[:], COPY)
+            nc.vector.tensor_single_scalar(pos[:], v[:], 0.0, IS_GT)
+            nc.vector.tensor_tensor(window[c][:].indirect(offsets[:]), v[:], pos[:], MULT)
+            nc.sync.dma_start(out[c * P : (c + 1) * P, :], window[c][:])

@@ -38,12 +38,12 @@ def times_weights(nc, held, banks, z, w, name):
     return y
 
 
-def times_adjacency(nc, banks, y, adj, block, half):
+def times_adjacency(nc, banks, y_blocks, adj, half):
     acc = banks.tile([P, BANK], F32, name="acc")
     for m in range(N // P):
         nc.tensor.matmul(
             acc[:],
-            y[m][:, block * P : (block + 1) * P],
+            y_blocks[m],
             adj[m][:, half * BANK : (half + 1) * BANK],
             start=(m == 0),
             stop=(m == N // P - 1),
@@ -56,7 +56,7 @@ def hidden_layer(nc, held, banks, z, w, adj, name):
     z_next = [held.tile([P, N], BF16, name=f"z{name}_{h}") for h in range(H // P)]
     for half in range(N // BANK):
         for h in range(H // P):
-            acc = times_adjacency(nc, banks, y, adj, h, half)
+            acc = times_adjacency(nc, banks, [y_m[:, h * P : (h + 1) * P] for y_m in y], adj, half)
             leave_psum(nc, h, z_next[h][:, half * BANK : (half + 1) * BANK], acc[:], relu=True)
     return z_next
 
@@ -80,14 +80,30 @@ def tile_gae_b_kernel(tc, base, x, adj_t, w1, w2, w3, offs, out):
 
         z1 = hidden_layer(nc, held, banks, x_k, w1_k, adj, "1")
         z2 = hidden_layer(nc, held, banks, z1, w2_k, adj, "2")
-        y3 = times_weights(nc, held, banks, z2, w3_k, "y3_")
 
         for c in range(C // P):
+            y3 = []
+            for first in range(0, N // P, BANK // P):
+                acc = banks.tile([P, BANK], F32, name="acc")
+                for i in range(BANK // P):
+                    for k in range(H // P):
+                        nc.tensor.matmul(
+                            acc[:, i * P : (i + 1) * P],
+                            z2[k][:, (first + i) * P : (first + i + 1) * P],
+                            w3_k[k][:, c * P : (c + 1) * P],
+                            start=(k == 0),
+                            stop=(k == H // P - 1),
+                        )
+                y3_four = held.tile([P, BANK], BF16, name=f"y3_{c}_{first}")
+                nc.scalar.activation(y3_four[:], acc[:], COPY)
+                y3 += [y3_four[:, i * P : (i + 1) * P] for i in range(BANK // P)]
+
             v = held.tile([P, N], F32, name=f"v{c}")
             pos = held.tile([P, N], F32, name=f"pos{c}")
             for half in range(N // BANK):
-                acc = times_adjacency(nc, banks, y3, adj, c, half)
-                nc.scalar.activation(v[:, half * BANK : (half + 1) * BANK], acc[:], COPY)
-            nc.vector.tensor_single_scalar(pos[:], v[:], 0.0, IS_GT)
+                cols = slice(half * BANK, (half + 1) * BANK)
+                acc = times_adjacency(nc, banks, y3, adj, half)
+                nc.scalar.activation(v[:, cols], acc[:], COPY)
+                nc.vector.tensor_single_scalar(pos[:, cols], v[:, cols], 0.0, IS_GT)
             nc.vector.tensor_tensor(window[c][:].indirect(offsets[:]), v[:], pos[:], MULT)
             nc.sync.dma_start(out[c * P : (c + 1) * P, :], window[c][:])

@@ -25,16 +25,18 @@ def leave_psum(nc, turn, dest, bank, relu):
         nc.vector.tensor_copy(dest, bank)
 
 
-def times_weights(nc, held, banks, z, w, name):
-    width = w[0].shape[1]
+def times_weights(nc, held, banks, z, w, together, name):
     y = []
-    for m in range(N // P):
-        acc = banks.tile([P, width], F32, name="acc")
+    for first in range(0, N // P, together):
+        accs = [banks.tile([P, H], F32, name="acc") for m in range(together)]
         for k in range(len(z)):
-            nc.tensor.matmul(acc[:], z[k][:, m * P : (m + 1) * P], w[k][:], start=(k == 0), stop=(k == len(z) - 1))
-        y_m = held.tile([P, width], BF16, name=f"{name}{m}")
-        leave_psum(nc, m, y_m[:], acc[:], relu=False)
-        y.append(y_m)
+            for i in range(together):
+                m = first + i
+                nc.tensor.matmul(accs[i][:], z[k][:, m * P : (m + 1) * P], w[k][:], start=(k == 0), stop=(k == len(z) - 1))
+        for i in range(together):
+            y_m = held.tile([P, H], BF16, name=f"{name}{first + i}")
+            leave_psum(nc, i, y_m[:], accs[i][:], relu=False)
+            y.append(y_m)
     return y
 
 
@@ -51,8 +53,8 @@ def times_adjacency(nc, banks, y_blocks, adj, half):
     return acc
 
 
-def hidden_layer(nc, held, banks, z, w, adj, name):
-    y = times_weights(nc, held, banks, z, w, f"y{name}_")
+def hidden_layer(nc, held, banks, z, w, adj, together, name):
+    y = times_weights(nc, held, banks, z, w, together, f"y{name}_")
     z_next = [held.tile([P, N], BF16, name=f"z{name}_{h}") for h in range(H // P)]
     for half in range(N // BANK):
         for h in range(H // P):
@@ -78,8 +80,8 @@ def tile_gae_b_kernel(tc, base, x, adj_t, w1, w2, w3, offs, out):
         w3_k = [load_row_block(nc, held, w3, k, "w3_") for k in range(H // P)]
         window = [load_row_block(nc, held, base, c, "window") for c in range(C // P)]
 
-        z1 = hidden_layer(nc, held, banks, x_k, w1_k, adj, "1")
-        z2 = hidden_layer(nc, held, banks, z1, w2_k, adj, "2")
+        z1 = hidden_layer(nc, held, banks, x_k, w1_k, adj, N // P, "1")
+        z2 = hidden_layer(nc, held, banks, z1, w2_k, adj, 1, "2")
 
         for c in range(C // P):
             y3 = []

@@ -3,6 +3,7 @@ import concourse.mybir as mybir
 P = 128
 CIN, H, C, S, N = 1024, 512, 256, 4096, 1024
 BANK = 512
+WARM_UP = 4
 FLOPS = 2 * (N * CIN * H + H * N * N + N * H * H + H * N * N + N * H * C + C * N * N)
 
 BF16, F32, U16 = mybir.dt.bfloat16, mybir.dt.float32, mybir.dt.uint16
@@ -69,6 +70,12 @@ def tile_gae_b_kernel(tc, base, x, adj_t, w1, w2, w3, offs, out):
         tc.tile_pool(name="held", bufs=1) as held,
         tc.psum_pool(name="banks", bufs=8) as banks,
     ):
+        zeros = held.tile([P, BANK], BF16, name="zeros")
+        nc.vector.memset(zeros[:], 0.0)
+        idle = banks.tile([P, BANK], F32, name="acc")
+        for i in range(WARM_UP):
+            nc.tensor.matmul(idle[:], zeros[:, 0:P], zeros[:], start=True, stop=True)
+
         offsets = held.tile([P, N // 16], U16, name="offsets")
         nc.sync.dma_start(offsets[:], offs)
         x_k, w1_k = [], []

@@ -114,5 +114,6 @@ def tile_gae_b_kernel(tc, base, x, adj_t, w1, w2, w3, offs, out):
                 acc = times_adjacency(nc, banks, y3, adj, half)
                 nc.scalar.activation(v[:, cols], acc[:], COPY)
                 nc.vector.tensor_single_scalar(pos[:, cols], v[:, cols], 0.0, IS_GT)
-            nc.vector.tensor_tensor(window[c][:].indirect(offsets[:]), v[:], pos[:], MULT)
+                listed = offsets[:, half * (BANK // 16) : (half + 1) * (BANK // 16)]
+                nc.vector.tensor_tensor(window[c][:].indirect(listed), v[:, cols], pos[:, cols], MULT)
             nc.sync.dma_start(out[c * P : (c + 1) * P, :], window[c][:])

@@ -3,11 +3,11 @@ import concourse.mybir as mybir
 P = 128
 CIN, H, C, S, N = 1024, 512, 256, 4096, 1024
 BANK = 512
-WARM_UP = 4
+WARM_UP = 3
 FLOPS = 2 * (N * CIN * H + H * N * N + N * H * H + H * N * N + N * H * C + C * N * N)
 
 BF16, F32, U16 = mybir.dt.bfloat16, mybir.dt.float32, mybir.dt.uint16
-COPY, RELU = mybir.ActivationFunctionType.Copy, mybir.ActivationFunctionType.Relu
+COPY, RELU, SIGN = (mybir.ActivationFunctionType.Copy, mybir.ActivationFunctionType.Relu, mybir.ActivationFunctionType.Sign)
 MULT, IS_GT = mybir.AluOpType.mult, mybir.AluOpType.is_gt
 
 
@@ -76,15 +76,19 @@ def tile_gae_b_kernel(tc, base, x, adj_t, w1, w2, w3, offs, out):
         for i in range(WARM_UP):
             nc.tensor.matmul(idle[:], zeros[:, 0:P], zeros[:], start=True, stop=True)
 
-        offsets = held.tile([P, N // 16], U16, name="offsets")
-        nc.sync.dma_start(offsets[:], offs)
         x_k, w1_k = [], []
         for k in range(CIN // P):
-            x_k.append(load_row_block(nc, held, x, k, "x"))
             w1_k.append(load_row_block(nc, held, w1, k, "w1_"))
+            x_rows = held.tile([P, N], BF16, name=f"x{k}")
+            for half in range(N // BANK):
+                cols = slice(half * BANK, (half + 1) * BANK)
+                nc.sync.dma_start(x_rows[:, cols], x[k * P : (k + 1) * P, cols])
+            x_k.append(x_rows)
         adj = [load_row_block(nc, held, adj_t, m, "adj") for m in range(N // P)]
         w2_k = [load_row_block(nc, held, w2, k, "w2_") for k in range(H // P)]
         w3_k = [load_row_block(nc, held, w3, k, "w3_") for k in range(H // P)]
+        offsets = held.tile([P, N // 16], U16, name="offsets")
+        nc.sync.dma_start(offsets[:], offs)
         window = [load_row_block(nc, held, base, c, "window") for c in range(C // P)]
 
         z1 = hidden_layer(nc, held, banks, x_k, w1_k, adj, N // P, "1")
@@ -109,11 +113,16 @@ def tile_gae_b_kernel(tc, base, x, adj_t, w1, w2, w3, offs, out):
 
             v = held.tile([P, N], F32, name=f"v{c}")
             pos = held.tile([P, N], F32, name=f"pos{c}")
+            above = held.tile([P, N], F32, name=f"above{c}")
             for half in range(N // BANK):
                 cols = slice(half * BANK, (half + 1) * BANK)
                 acc = times_adjacency(nc, banks, y3, adj, half)
                 nc.scalar.activation(v[:, cols], acc[:], COPY)
-                nc.vector.tensor_single_scalar(pos[:, cols], v[:, cols], 0.0, IS_GT)
+                if half == 0:
+                    nc.vector.tensor_single_scalar(pos[:, cols], v[:, cols], 0.0, IS_GT)
+                else:
+                    nc.scalar.activation(above[:, cols], acc[:], RELU)
+                    nc.scalar.activation(pos[:, cols], above[:, cols], SIGN)
                 listed = offsets[:, half * (BANK // 16) : (half + 1) * (BANK // 16)]
                 nc.vector.tensor_tensor(window[c][:].indirect(listed), v[:, cols], pos[:, cols], MULT)
             nc.sync.dma_start(out[c * P : (c + 1) * P, :], window[c][:])

@@ -9,6 +9,7 @@ FLOPS = 2 * (N * CIN * H + H * N * N + N * H * H + H * N * N + N * H * C + C * N
 BF16, F32, U16 = mybir.dt.bfloat16, mybir.dt.float32, mybir.dt.uint16
 COPY, RELU, SIGN = (mybir.ActivationFunctionType.Copy, mybir.ActivationFunctionType.Relu, mybir.ActivationFunctionType.Sign)
 MULT, IS_GT = mybir.AluOpType.mult, mybir.AluOpType.is_gt
+SCALAR, VECTOR = 0, 1
 
 
 def load_row_block(nc, pool, matrix, block, name):
@@ -108,7 +109,7 @@ def tile_gae_b_kernel(tc, base, x, adj_t, w1, w2, w3, offs, out):
                             stop=(k == H // P - 1),
                         )
                 y3_four = held.tile([P, BANK], BF16, name=f"y3_{c}_{first}")
-                nc.scalar.activation(y3_four[:], acc[:], COPY)
+                leave_psum(nc, VECTOR if c == 0 else SCALAR, y3_four[:], acc[:], relu=False)
                 y3 += [y3_four[:, i * P : (i + 1) * P] for i in range(BANK // P)]
 
             v = held.tile([P, N], F32, name=f"v{c}")
@@ -117,7 +118,7 @@ def tile_gae_b_kernel(tc, base, x, adj_t, w1, w2, w3, offs, out):
             for half in range(N // BANK):
                 cols = slice(half * BANK, (half + 1) * BANK)
                 acc = times_adjacency(nc, banks, y3, adj, half)
-                nc.scalar.activation(v[:, cols], acc[:], COPY)
+                leave_psum(nc, VECTOR if c == 0 and half == 0 else SCALAR, v[:, cols], acc[:], relu=False)
                 if half == 0:
                     nc.vector.tensor_single_scalar(pos[:, cols], v[:, cols], 0.0, IS_GT)
                 else:

@@ -3,6 +3,7 @@ import concourse.mybir as mybir
 P = 128
 CIN, H, C, S, N = 1024, 512, 256, 4096, 1024
 BANK = 512
+PAIR = 2
 WARM_UP = 3
 FLOPS = 2 * (N * CIN * H + H * N * N + N * H * H + H * N * N + N * H * C + C * N * N)
 
@@ -42,16 +43,10 @@ def times_weights(nc, held, banks, z, w, together, name):
     return y
 
 
-def times_adjacency(nc, banks, y_blocks, adj, half):
-    acc = banks.tile([P, BANK], F32, name="acc")
+def times_adjacency(nc, banks, y_blocks, adj, cols):
+    acc = banks.tile([P, cols.stop - cols.start], F32, name="acc")
     for m in range(N // P):
-        nc.tensor.matmul(
-            acc[:],
-            y_blocks[m],
-            adj[m][:, half * BANK : (half + 1) * BANK],
-            start=(m == 0),
-            stop=(m == N // P - 1),
-        )
+        nc.tensor.matmul(acc[:], y_blocks[m], adj[m][:, cols], start=(m == 0), stop=(m == N // P - 1))
     return acc
 
 
@@ -60,8 +55,9 @@ def hidden_layer(nc, held, banks, z, w, adj, together, name):
     z_next = [held.tile([P, N], BF16, name=f"z{name}_{h}") for h in range(H // P)]
     for half in range(N // BANK):
         for h in range(H // P):
-            acc = times_adjacency(nc, banks, [y_m[:, h * P : (h + 1) * P] for y_m in y], adj, half)
-            leave_psum(nc, h, z_next[h][:, half * BANK : (half + 1) * BANK], acc[:], relu=True)
+            cols = slice(half * BANK, (half + 1) * BANK)
+            acc = times_adjacency(nc, banks, [y_m[:, h * P : (h + 1) * P] for y_m in y], adj, cols)
+            leave_psum(nc, h, z_next[h][:, cols], acc[:], relu=True)
     return z_next
 
 
@@ -97,9 +93,9 @@ def tile_gae_b_kernel(tc, base, x, adj_t, w1, w2, w3, offs, out):
 
         for c in range(C // P):
             y3 = []
-            for first in range(0, N // P, BANK // P):
-                acc = banks.tile([P, BANK], F32, name="acc")
-                for i in range(BANK // P):
+            for first in range(0, N // P, PAIR):
+                acc = banks.tile([P, PAIR * P], F32, name="acc")
+                for i in range(PAIR):
                     for k in range(H // P):
                         nc.tensor.matmul(
                             acc[:, i * P : (i + 1) * P],
@@ -108,22 +104,25 @@ def tile_gae_b_kernel(tc, base, x, adj_t, w1, w2, w3, offs, out):
                             start=(k == 0),
                             stop=(k == H // P - 1),
                         )
-                y3_four = held.tile([P, BANK], BF16, name=f"y3_{c}_{first}")
-                leave_psum(nc, VECTOR if c == 0 else SCALAR, y3_four[:], acc[:], relu=False)
-                y3 += [y3_four[:, i * P : (i + 1) * P] for i in range(BANK // P)]
+                y3_pair = held.tile([P, PAIR * P], BF16, name=f"y3_{c}_{first}")
+                leave_psum(nc, VECTOR if c == 0 else SCALAR, y3_pair[:], acc[:], relu=False)
+                y3 += [y3_pair[:, i * P : (i + 1) * P] for i in range(PAIR)]
 
             v = held.tile([P, N], F32, name=f"v{c}")
             pos = held.tile([P, N], F32, name=f"pos{c}")
             above = held.tile([P, N], F32, name=f"above{c}")
             for half in range(N // BANK):
-                cols = slice(half * BANK, (half + 1) * BANK)
-                acc = times_adjacency(nc, banks, y3, adj, half)
-                leave_psum(nc, VECTOR if c == 0 and half == 0 else SCALAR, v[:, cols], acc[:], relu=False)
-                if half == 0:
-                    nc.vector.tensor_single_scalar(pos[:, cols], v[:, cols], 0.0, IS_GT)
-                else:
-                    nc.scalar.activation(above[:, cols], acc[:], RELU)
-                    nc.scalar.activation(pos[:, cols], above[:, cols], SIGN)
-                listed = offsets[:, half * (BANK // 16) : (half + 1) * (BANK // 16)]
-                nc.vector.tensor_tensor(window[c][:].indirect(listed), v[:, cols], pos[:, cols], MULT)
+                piece = slice(half * BANK, (half + 1) * BANK)
+                width = BANK // 2 if half == 0 else BANK
+                for start in range(piece.start, piece.stop, width):
+                    cols = slice(start, start + width)
+                    acc = times_adjacency(nc, banks, y3, adj, cols)
+                    leave_psum(nc, VECTOR if c == 0 and half == 0 else SCALAR, v[:, cols], acc[:], relu=False)
+                    if half == 0:
+                        nc.vector.tensor_single_scalar(pos[:, cols], v[:, cols], 0.0, IS_GT)
+                    else:
+                        nc.scalar.activation(above[:, cols], acc[:], RELU)
+                        nc.scalar.activation(pos[:, cols], above[:, cols], SIGN)
+                listed = offsets[:, piece.start // 16 : piece.stop // 16]
+                nc.vector.tensor_tensor(window[c][:].indirect(listed), v[:, piece], pos[:, piece], MULT)
             nc.sync.dma_start(out[c * P : (c + 1) * P, :], window[c][:])

@@ -113,12 +113,11 @@ def tile_gae_b_kernel(tc, base, x, adj_t, w1, w2, w3, offs, out):
             above = held.tile([P, N], F32, name=f"above{c}")
             for half in range(N // BANK):
                 piece = slice(half * BANK, (half + 1) * BANK)
-                width = BANK // 2 if half == 0 else BANK
-                for start in range(piece.start, piece.stop, width):
-                    cols = slice(start, start + width)
+                for start in range(piece.start, piece.stop, BANK // 2):
+                    cols = slice(start, start + BANK // 2)
                     acc = times_adjacency(nc, banks, y3, adj, cols)
                     leave_psum(nc, VECTOR if c == 0 and half == 0 else SCALAR, v[:, cols], acc[:], relu=False)
-                    if half == 0:
+                    if c == 0 and half == 0:
                         nc.vector.tensor_single_scalar(pos[:, cols], v[:, cols], 0.0, IS_GT)
                     else:
                         nc.scalar.activation(above[:, cols], acc[:], RELU)

@@ -116,11 +116,12 @@ def tile_gae_b_kernel(tc, base, x, adj_t, w1, w2, w3, offs, out):
                 for start in range(piece.start, piece.stop, BANK // 2):
                     cols = slice(start, start + BANK // 2)
                     acc = times_adjacency(nc, banks, y3, adj, cols)
-                    leave_psum(nc, VECTOR if c == 0 and half == 0 else SCALAR, v[:, cols], acc[:], relu=False)
                     if c == 0 and half == 0:
+                        leave_psum(nc, VECTOR, v[:, cols], acc[:], relu=False)
                         nc.vector.tensor_single_scalar(pos[:, cols], v[:, cols], 0.0, IS_GT)
                     else:
-                        nc.scalar.activation(above[:, cols], acc[:], RELU)
+                        leave_psum(nc, SCALAR, above[:, cols], acc[:], relu=True)
+                        leave_psum(nc, SCALAR, v[:, cols], acc[:], relu=False)
                         nc.scalar.activation(pos[:, cols], above[:, cols], SIGN)
                 listed = offsets[:, piece.start // 16 : piece.stop // 16]
                 nc.vector.tensor_tensor(window[c][:].indirect(listed), v[:, piece], pos[:, piece], MULT)

@@ -113,12 +113,13 @@ def tile_gae_b_kernel(tc, base, x, adj_t, w1, w2, w3, offs, out):
             above = held.tile([P, N], F32, name=f"above{c}")
             for half in range(N // BANK):
                 piece = slice(half * BANK, (half + 1) * BANK)
-                for start in range(piece.start, piece.stop, BANK // 2):
-                    cols = slice(start, start + BANK // 2)
+                starts = [0, BANK // 2, BANK * 3 // 4, BANK] if c == 0 and half == 0 else [0, BANK // 2, BANK]
+                for first, last in zip(starts[:-1], starts[1:]):
+                    cols = slice(piece.start + first, piece.start + last)
                     acc = times_adjacency(nc, banks, y3, adj, cols)
                     if c == 0 and half == 0:
                         leave_psum(nc, VECTOR, v[:, cols], acc[:], relu=False)
-                        nc.vector.tensor_single_scalar(pos[:, cols], v[:, cols], 0.0, IS_GT)
+                        nc.vector.tensor_single_scalar(pos[:, cols], acc[:], 0.0, IS_GT)
                     else:
                         leave_psum(nc, SCALAR, above[:, cols], acc[:], relu=True)
                         leave_psum(nc, SCALAR, v[:, cols], acc[:], relu=False)

import concourse.mybir as mybir

P = 128
CIN, H, C, S, N = 1024, 512, 256, 4096, 1024
BANK = 512
PAIR = 2
WARM_UP = 3
FLOPS = 2 * (N * CIN * H + H * N * N + N * H * H + H * N * N + N * H * C + C * N * N)

BF16, F32, U16 = mybir.dt.bfloat16, mybir.dt.float32, mybir.dt.uint16
COPY, RELU, SIGN = (mybir.ActivationFunctionType.Copy, mybir.ActivationFunctionType.Relu, mybir.ActivationFunctionType.Sign)
MULT, IS_GT = mybir.AluOpType.mult, mybir.AluOpType.is_gt
SCALAR, VECTOR = 0, 1


def load_row_block(nc, pool, matrix, block, name):
    rows = pool.tile([P, matrix.shape[1]], matrix.dtype, name=f"{name}{block}")
    nc.sync.dma_start(rows[:], matrix[block * P : (block + 1) * P, :])
    return rows


def leave_psum(nc, turn, dest, bank, relu):
    if turn % 2 == 0:
        nc.scalar.activation(dest, bank, RELU if relu else COPY)
    elif relu:
        nc.vector.tensor_scalar_max(dest, bank, 0.0)
    else:
        nc.vector.tensor_copy(dest, bank)


def times_weights(nc, held, banks, z, w, together, name):
    y = []
    for first in range(0, N // P, together):
        accs = [banks.tile([P, H], F32, name="acc") for m in range(together)]
        for k in range(len(z)):
            for i in range(together):
                m = first + i
                nc.tensor.matmul(accs[i][:], z[k][:, m * P : (m + 1) * P], w[k][:], start=(k == 0), stop=(k == len(z) - 1))
        for i in range(together):
            y_m = held.tile([P, H], BF16, name=f"{name}{first + i}")
            leave_psum(nc, i, y_m[:], accs[i][:], relu=False)
            y.append(y_m)
    return y


def times_adjacency(nc, banks, y_blocks, adj, cols):
    acc = banks.tile([P, cols.stop - cols.start], F32, name="acc")
    for m in range(N // P):
        nc.tensor.matmul(acc[:], y_blocks[m], adj[m][:, cols], start=(m == 0), stop=(m == N // P - 1))
    return acc


def hidden_layer(nc, held, banks, z, w, adj, together, name):
    y = times_weights(nc, held, banks, z, w, together, f"y{name}_")
    z_next = [held.tile([P, N], BF16, name=f"z{name}_{h}") for h in range(H // P)]
    for half in range(N // BANK):
        for h in range(H // P):
            cols = slice(half * BANK, (half + 1) * BANK)
            acc = times_adjacency(nc, banks, [y_m[:, h * P : (h + 1) * P] for y_m in y], adj, cols)
            leave_psum(nc, h, z_next[h][:, cols], acc[:], relu=True)
    return z_next


def tile_gae_b_kernel(tc, base, x, adj_t, w1, w2, w3, offs, out):
    nc = tc.nc
    with (
        tc.tile_pool(name="held", bufs=1) as held,
        tc.psum_pool(name="banks", bufs=8) as banks,
    ):
        zeros = held.tile([P, BANK], BF16, name="zeros")
        nc.vector.memset(zeros[:], 0.0)
        idle = banks.tile([P, BANK], F32, name="acc")
        for i in range(WARM_UP):
            nc.tensor.matmul(idle[:], zeros[:, 0:P], zeros[:], start=True, stop=True)

        x_k, w1_k = [], []
        for k in range(CIN // P):
            w1_k.append(load_row_block(nc, held, w1, k, "w1_"))
            x_rows = held.tile([P, N], BF16, name=f"x{k}")
            for half in range(N // BANK):
                cols = slice(half * BANK, (half + 1) * BANK)
                nc.sync.dma_start(x_rows[:, cols], x[k * P : (k + 1) * P, cols])
            x_k.append(x_rows)
        adj = [load_row_block(nc, held, adj_t, m, "adj") for m in range(N // P)]
        w2_k = [load_row_block(nc, held, w2, k, "w2_") for k in range(H // P)]
        w3_k = [load_row_block(nc, held, w3, k, "w3_") for k in range(H // P)]
        offsets = held.tile([P, N // 16], U16, name="offsets")
        nc.sync.dma_start(offsets[:], offs)
        window = [load_row_block(nc, held, base, c, "window") for c in range(C // P)]

        z1 = hidden_layer(nc, held, banks, x_k, w1_k, adj, N // P, "1")
        z2 = hidden_layer(nc, held, banks, z1, w2_k, adj, 1, "2")

        for c in range(C // P):
            y3 = []
            for first in range(0, N // P, PAIR):
                acc = banks.tile([P, PAIR * P], F32, name="acc")
                for i in range(PAIR):
                    for k in range(H // P):
                        nc.tensor.matmul(
                            acc[:, i * P : (i + 1) * P],
                            z2[k][:, (first + i) * P : (first + i + 1) * P],
                            w3_k[k][:, c * P : (c + 1) * P],
                            start=(k == 0),
                            stop=(k == H // P - 1),
                        )
                y3_pair = held.tile([P, PAIR * P], BF16, name=f"y3_{c}_{first}")
                leave_psum(nc, VECTOR if c == 0 else SCALAR, y3_pair[:], acc[:], relu=False)
                y3 += [y3_pair[:, i * P : (i + 1) * P] for i in range(PAIR)]

            v = held.tile([P, N], F32, name=f"v{c}")
            pos = held.tile([P, N], F32, name=f"pos{c}")
            above = held.tile([P, N], F32, name=f"above{c}")
            for half in range(N // BANK):
                piece = slice(half * BANK, (half + 1) * BANK)
                starts = [0, BANK // 2, BANK * 3 // 4, BANK] if c == 0 and half == 0 else [0, BANK // 2, BANK]
                for first, last in zip(starts[:-1], starts[1:]):
                    cols = slice(piece.start + first, piece.start + last)
                    acc = times_adjacency(nc, banks, y3, adj, cols)
                    if c == 0 and half == 0:
                        leave_psum(nc, VECTOR, v[:, cols], acc[:], relu=False)
                        nc.vector.tensor_single_scalar(pos[:, cols], acc[:], 0.0, IS_GT)
                    else:
                        leave_psum(nc, SCALAR, above[:, cols], acc[:], relu=True)
                        leave_psum(nc, SCALAR, v[:, cols], acc[:], relu=False)
                        nc.scalar.activation(pos[:, cols], above[:, cols], SIGN)
                listed = offsets[:, piece.start // 16 : piece.stop // 16]
                nc.vector.tensor_tensor(window[c][:].indirect(listed), v[:, piece], pos[:, piece], MULT)
            nc.sync.dma_start(out[c * P : (c + 1) * P, :], window[c][:])
